import numpy as np
import ml_dtypes

BF16 = ml_dtypes.bfloat16


def bf(x):
    return np.asarray(x, np.float32).astype(BF16)


def f32(x):
    return np.asarray(x, np.float32)


def f64(x):
    return np.asarray(x).astype(np.float64)


def striped(idx):
    return np.tile(idx.reshape(-1, 16).T, (8, 1))


D, S, M, N = 128, 512, 512, 256
TEMPERATURE = 0.1


def setup_inputs():
    return {"table": bf(np.random.standard_normal((D, S)) / np.sqrt(D)), "w": bf(np.random.standard_normal((D, M)) / np.sqrt(D)), "offs": striped(np.random.permutation(np.tile(np.arange(S), 2))[:N])}


def reference(table, w, offs):
    idx = offs[:16].T.reshape(-1)
    z = (f64(w).T @ f64(table)[:, idx]) / TEMPERATURE
    return z - np.max(z, axis=1, keepdims=True)

@@ -1,0 +1,50 @@
+import concourse.mybir as mybir
+
+P = 128
+CLASSES = 512
+PIXELS = 512
+ANCHORS = 256
+BLOCKS = PIXELS // P
+INV_TEMPERATURE = 10.0
+
+FLOPS = 2 * P * PIXELS * ANCHORS
+
+BF16, F32, U16 = mybir.dt.bfloat16, mybir.dt.float32, mybir.dt.uint16
+
+
+def tile_pixelcontrastloss_kernel(tc, table, w, offs, out):
+    nc = tc.nc
+    with (
+        tc.tile_pool(name="held", bufs=1) as held,
+        tc.tile_pool(name="rows", bufs=BLOCKS) as rows,
+        tc.psum_pool(name="psum", bufs=BLOCKS) as psum,
+    ):
+        offsets = held.tile([P, ANCHORS // 16], U16, name="offsets")
+        prototypes = held.tile([P, CLASSES], BF16, name="prototypes")
+        pixels = held.tile([P, PIXELS], BF16, name="pixels")
+        nc.sync.dma_start(offsets[:], offs)
+        nc.sync.dma_start(prototypes[:], table)
+        nc.scalar.dma_start(pixels[:], w)
+
+        for b in range(BLOCKS):
+            product = psum.tile([P, ANCHORS], F32, name="product")
+            nc.tensor.matmul(
+                product[:],
+                pixels[:, b * P : (b + 1) * P],
+                prototypes[:].indirect(offsets[:]),
+                start=True,
+                stop=True,
+            )
+
+            largest = rows.tile([P, 1], F32, name="largest")
+            nc.vector.reduce_max(largest[:], product[:], axis=mybir.AxisListType.X)
+            shifted = rows.tile([P, ANCHORS], F32, name="shifted")
+            nc.vector.tensor_scalar(
+                shifted[:],
+                product[:],
+                largest[:],
+                INV_TEMPERATURE,
+                op0=mybir.AluOpType.subtract,
+                op1=mybir.AluOpType.mult,
+            )
+            nc.sync.dma_start(out[b * P : (b + 1) * P, :], shifted[:])

@@ -6,6 +6,8 @@ PIXELS = 512
 ANCHORS = 256
 BLOCKS = PIXELS // P
 INV_TEMPERATURE = 10.0
+WARMUP = 4
+BANK = 512
 
 FLOPS = 2 * P * PIXELS * ANCHORS
 
@@ -18,6 +20,7 @@ def tile_pixelcontrastloss_kernel(tc, table, w, offs, out):
         tc.tile_pool(name="held", bufs=1) as held,
         tc.tile_pool(name="rows", bufs=BLOCKS) as rows,
         tc.psum_pool(name="psum", bufs=BLOCKS) as psum,
+        tc.psum_pool(name="idle", bufs=1) as idle,
     ):
         offsets = held.tile([P, ANCHORS // 16], U16, name="offsets")
         prototypes = held.tile([P, CLASSES], BF16, name="prototypes")
@@ -25,6 +28,12 @@ def tile_pixelcontrastloss_kernel(tc, table, w, offs, out):
         nc.sync.dma_start(offsets[:], offs)
         nc.sync.dma_start(prototypes[:], table)
         nc.scalar.dma_start(pixels[:], w)
+
+        zeros = held.tile([P, BANK], BF16, name="zeros")
+        nc.vector.memset(zeros[:], 0.0)
+        unused = idle.tile([P, BANK], F32, name="unused")
+        for i in range(WARMUP):
+            nc.tensor.matmul(unused[:], zeros[:, 0:P], zeros[:], start=True, stop=True)
 
         for b in range(BLOCKS):
             product = psum.tile([P, ANCHORS], F32, name="product")

@@ -6,8 +6,6 @@ PIXELS = 512
 ANCHORS = 256
 BLOCKS = PIXELS // P
 INV_TEMPERATURE = 10.0
-WARMUP = 4
-BANK = 512
 
 FLOPS = 2 * P * PIXELS * ANCHORS
 
@@ -20,7 +18,6 @@ def tile_pixelcontrastloss_kernel(tc, table, w, offs, out):
         tc.tile_pool(name="held", bufs=1) as held,
         tc.tile_pool(name="rows", bufs=BLOCKS) as rows,
         tc.psum_pool(name="psum", bufs=BLOCKS) as psum,
-        tc.psum_pool(name="idle", bufs=1) as idle,
     ):
         offsets = held.tile([P, ANCHORS // 16], U16, name="offsets")
         prototypes = held.tile([P, CLASSES], BF16, name="prototypes")
@@ -28,12 +25,6 @@ def tile_pixelcontrastloss_kernel(tc, table, w, offs, out):
         nc.sync.dma_start(offsets[:], offs)
         nc.sync.dma_start(prototypes[:], table)
         nc.scalar.dma_start(pixels[:], w)
-
-        zeros = held.tile([P, BANK], BF16, name="zeros")
-        nc.vector.memset(zeros[:], 0.0)
-        unused = idle.tile([P, BANK], F32, name="unused")
-        for i in range(WARMUP):
-            nc.tensor.matmul(unused[:], zeros[:, 0:P], zeros[:], start=True, stop=True)
 
         for b in range(BLOCKS):
             product = psum.tile([P, ANCHORS], F32, name="product")
@@ -47,13 +38,14 @@ def tile_pixelcontrastloss_kernel(tc, table, w, offs, out):
 
             largest = rows.tile([P, 1], F32, name="largest")
             nc.vector.reduce_max(largest[:], product[:], axis=mybir.AxisListType.X)
+            shift = rows.tile([P, 1], F32, name="shift")
+            nc.vector.tensor_scalar(shift[:], largest[:], -INV_TEMPERATURE, None, op0=mybir.AluOpType.mult)
             shifted = rows.tile([P, ANCHORS], F32, name="shifted")
-            nc.vector.tensor_scalar(
+            nc.scalar.activation(
                 shifted[:],
                 product[:],
-                largest[:],
-                INV_TEMPERATURE,
-                op0=mybir.AluOpType.subtract,
-                op1=mybir.AluOpType.mult,
+                mybir.ActivationFunctionType.Identity,
+                bias=shift[:],
+                scale=INV_TEMPERATURE,
             )
-            nc.sync.dma_start(out[b * P : (b + 1) * P, :], shifted[:])
+            nc.scalar.dma_start(out[b * P : (b + 1) * P, :], shifted[:])

@@ -48,4 +48,4 @@ def tile_pixelcontrastloss_kernel(tc, table, w, offs, out):
                 bias=shift[:],
                 scale=INV_TEMPERATURE,
             )
-            nc.scalar.dma_start(out[b * P : (b + 1) * P, :], shifted[:])
+            nc.sync.dma_start(out[b * P : (b + 1) * P, :], shifted[:])

@@ -6,6 +6,8 @@ PIXELS = 512
 ANCHORS = 256
 BLOCKS = PIXELS // P
 INV_TEMPERATURE = 10.0
+BANK = 512
+WARMUP = 3
 
 FLOPS = 2 * P * PIXELS * ANCHORS
 
@@ -18,6 +20,7 @@ def tile_pixelcontrastloss_kernel(tc, table, w, offs, out):
         tc.tile_pool(name="held", bufs=1) as held,
         tc.tile_pool(name="rows", bufs=BLOCKS) as rows,
         tc.psum_pool(name="psum", bufs=BLOCKS) as psum,
+        tc.psum_pool(name="idle", bufs=1) as idle,
     ):
         offsets = held.tile([P, ANCHORS // 16], U16, name="offsets")
         prototypes = held.tile([P, CLASSES], BF16, name="prototypes")
@@ -25,6 +28,12 @@ def tile_pixelcontrastloss_kernel(tc, table, w, offs, out):
         nc.sync.dma_start(offsets[:], offs)
         nc.sync.dma_start(prototypes[:], table)
         nc.scalar.dma_start(pixels[:], w)
+
+        zeros = held.tile([P, BANK], BF16, name="zeros")
+        nc.vector.memset(zeros[:], 0.0)
+        unused = idle.tile([P, BANK], F32, name="unused")
+        for i in range(WARMUP):
+            nc.tensor.matmul(unused[:], zeros[:, 0:P], zeros[:], start=True, stop=True)
 
         for b in range(BLOCKS):
             product = psum.tile([P, ANCHORS], F32, name="product")
@@ -36,16 +45,23 @@ def tile_pixelcontrastloss_kernel(tc, table, w, offs, out):
                 stop=True,
             )
 
-            largest = rows.tile([P, 1], F32, name="largest")
-            nc.vector.reduce_max(largest[:], product[:], axis=mybir.AxisListType.X)
+            negated = rows.tile([P, ANCHORS], F32, name="negated")
             shift = rows.tile([P, 1], F32, name="shift")
-            nc.vector.tensor_scalar(shift[:], largest[:], -INV_TEMPERATURE, None, op0=mybir.AluOpType.mult)
+            nc.vector.tensor_scalar(
+                negated[:],
+                product[:],
+                -INV_TEMPERATURE,
+                None,
+                op0=mybir.AluOpType.mult,
+                op1=mybir.AluOpType.min,
+                accum_out=shift[:],
+            )
             shifted = rows.tile([P, ANCHORS], F32, name="shifted")
             nc.scalar.activation(
                 shifted[:],
-                product[:],
+                negated[:],
                 mybir.ActivationFunctionType.Identity,
                 bias=shift[:],
-                scale=INV_TEMPERATURE,
+                scale=-1.0,
             )
             nc.sync.dma_start(out[b * P : (b + 1) * P, :], shifted[:])

@@ -6,8 +6,6 @@ PIXELS = 512
 ANCHORS = 256
 BLOCKS = PIXELS // P
 INV_TEMPERATURE = 10.0
-BANK = 512
-WARMUP = 3
 
 FLOPS = 2 * P * PIXELS * ANCHORS
 
@@ -20,7 +18,6 @@ def tile_pixelcontrastloss_kernel(tc, table, w, offs, out):
         tc.tile_pool(name="held", bufs=1) as held,
         tc.tile_pool(name="rows", bufs=BLOCKS) as rows,
         tc.psum_pool(name="psum", bufs=BLOCKS) as psum,
-        tc.psum_pool(name="idle", bufs=1) as idle,
     ):
         offsets = held.tile([P, ANCHORS // 16], U16, name="offsets")
         prototypes = held.tile([P, CLASSES], BF16, name="prototypes")
@@ -28,12 +25,6 @@ def tile_pixelcontrastloss_kernel(tc, table, w, offs, out):
         nc.sync.dma_start(offsets[:], offs)
         nc.sync.dma_start(prototypes[:], table)
         nc.scalar.dma_start(pixels[:], w)
-
-        zeros = held.tile([P, BANK], BF16, name="zeros")
-        nc.vector.memset(zeros[:], 0.0)
-        unused = idle.tile([P, BANK], F32, name="unused")
-        for i in range(WARMUP):
-            nc.tensor.matmul(unused[:], zeros[:, 0:P], zeros[:], start=True, stop=True)
 
         for b in range(BLOCKS):
             product = psum.tile([P, ANCHORS], F32, name="product")
@@ -45,23 +36,17 @@ def tile_pixelcontrastloss_kernel(tc, table, w, offs, out):
                 stop=True,
             )
 
-            negated = rows.tile([P, ANCHORS], F32, name="negated")
-            shift = rows.tile([P, 1], F32, name="shift")
+            scaled = rows.tile([P, ANCHORS], F32, name="scaled")
+            largest = rows.tile([P, 1], F32, name="largest")
             nc.vector.tensor_scalar(
-                negated[:],
+                scaled[:],
                 product[:],
-                -INV_TEMPERATURE,
+                INV_TEMPERATURE,
                 None,
                 op0=mybir.AluOpType.mult,
-                op1=mybir.AluOpType.min,
-                accum_out=shift[:],
+                op1=mybir.AluOpType.max,
+                accum_out=largest[:],
             )
             shifted = rows.tile([P, ANCHORS], F32, name="shifted")
-            nc.scalar.activation(
-                shifted[:],
-                negated[:],
-                mybir.ActivationFunctionType.Identity,
-                bias=shift[:],
-                scale=-1.0,
-            )
+            nc.vector.tensor_scalar(shifted[:], scaled[:], largest[:], None, op0=mybir.AluOpType.subtract)
             nc.sync.dma_start(out[b * P : (b + 1) * P, :], shifted[:])

@@ -6,6 +6,7 @@ PIXELS = 512
 ANCHORS = 256
 BLOCKS = PIXELS // P
 INV_TEMPERATURE = 10.0
+WARMUP = 16
 
 FLOPS = 2 * P * PIXELS * ANCHORS
 
@@ -18,6 +19,7 @@ def tile_pixelcontrastloss_kernel(tc, table, w, offs, out):
         tc.tile_pool(name="held", bufs=1) as held,
         tc.tile_pool(name="rows", bufs=BLOCKS) as rows,
         tc.psum_pool(name="psum", bufs=BLOCKS) as psum,
+        tc.psum_pool(name="idle", bufs=1) as idle,
     ):
         offsets = held.tile([P, ANCHORS // 16], U16, name="offsets")
         prototypes = held.tile([P, CLASSES], BF16, name="prototypes")
@@ -25,6 +27,12 @@ def tile_pixelcontrastloss_kernel(tc, table, w, offs, out):
         nc.sync.dma_start(offsets[:], offs)
         nc.sync.dma_start(prototypes[:], table)
         nc.scalar.dma_start(pixels[:], w)
+
+        zeros = held.tile([P, P], BF16, name="zeros")
+        nc.vector.memset(zeros[:], 0.0)
+        unused = idle.tile([P, P], F32, name="unused")
+        for i in range(WARMUP):
+            nc.tensor.matmul(unused[:], zeros[:], zeros[:], start=True, stop=True)
 
         for b in range(BLOCKS):
             product = psum.tile([P, ANCHORS], F32, name="product")
@@ -36,17 +44,23 @@ def tile_pixelcontrastloss_kernel(tc, table, w, offs, out):
                 stop=True,
             )
 
-            scaled = rows.tile([P, ANCHORS], F32, name="scaled")
-            largest = rows.tile([P, 1], F32, name="largest")
+            negated = rows.tile([P, ANCHORS], F32, name="negated")
+            shift = rows.tile([P, 1], F32, name="shift")
             nc.vector.tensor_scalar(
-                scaled[:],
+                negated[:],
                 product[:],
-                INV_TEMPERATURE,
+                -INV_TEMPERATURE,
                 None,
                 op0=mybir.AluOpType.mult,
-                op1=mybir.AluOpType.max,
-                accum_out=largest[:],
+                op1=mybir.AluOpType.min,
+                accum_out=shift[:],
             )
             shifted = rows.tile([P, ANCHORS], F32, name="shifted")
-            nc.vector.tensor_scalar(shifted[:], scaled[:], largest[:], None, op0=mybir.AluOpType.subtract)
+            nc.scalar.activation(
+                shifted[:],
+                negated[:],
+                mybir.ActivationFunctionType.Identity,
+                bias=shift[:],
+                scale=-1.0,
+            )
             nc.sync.dma_start(out[b * P : (b + 1) * P, :], shifted[:])

@@ -6,7 +6,6 @@ PIXELS = 512
 ANCHORS = 256
 BLOCKS = PIXELS // P
 INV_TEMPERATURE = 10.0
-WARMUP = 16
 
 FLOPS = 2 * P * PIXELS * ANCHORS
 
@@ -19,7 +18,6 @@ def tile_pixelcontrastloss_kernel(tc, table, w, offs, out):
         tc.tile_pool(name="held", bufs=1) as held,
         tc.tile_pool(name="rows", bufs=BLOCKS) as rows,
         tc.psum_pool(name="psum", bufs=BLOCKS) as psum,
-        tc.psum_pool(name="idle", bufs=1) as idle,
     ):
         offsets = held.tile([P, ANCHORS // 16], U16, name="offsets")
         prototypes = held.tile([P, CLASSES], BF16, name="prototypes")
@@ -27,12 +25,6 @@ def tile_pixelcontrastloss_kernel(tc, table, w, offs, out):
         nc.sync.dma_start(offsets[:], offs)
         nc.sync.dma_start(prototypes[:], table)
         nc.scalar.dma_start(pixels[:], w)
-
-        zeros = held.tile([P, P], BF16, name="zeros")
-        nc.vector.memset(zeros[:], 0.0)
-        unused = idle.tile([P, P], F32, name="unused")
-        for i in range(WARMUP):
-            nc.tensor.matmul(unused[:], zeros[:], zeros[:], start=True, stop=True)
 
         for b in range(BLOCKS):
             product = psum.tile([P, ANCHORS], F32, name="product")

@@ -22,9 +22,10 @@ def tile_pixelcontrastloss_kernel(tc, table, w, offs, out):
         offsets = held.tile([P, ANCHORS // 16], U16, name="offsets")
         prototypes = held.tile([P, CLASSES], BF16, name="prototypes")
         pixels = held.tile([P, PIXELS], BF16, name="pixels")
-        nc.sync.dma_start(offsets[:], offs)
         nc.sync.dma_start(prototypes[:], table)
-        nc.scalar.dma_start(pixels[:], w)
+        nc.sync.dma_start(pixels[:, :P], w[:, :P])
+        nc.sync.dma_start(offsets[:], offs)
+        nc.sync.dma_start(pixels[:, P:], w[:, P:])
 
         for b in range(BLOCKS):
             product = psum.tile([P, ANCHORS], F32, name="product")

@@ -49,11 +49,21 @@ def tile_pixelcontrastloss_kernel(tc, table, w, offs, out):
                 accum_out=shift[:],
             )
             shifted = rows.tile([P, ANCHORS], F32, name="shifted")
-            nc.scalar.activation(
-                shifted[:],
-                negated[:],
-                mybir.ActivationFunctionType.Identity,
-                bias=shift[:],
-                scale=-1.0,
-            )
+            if b < BLOCKS - 1:
+                nc.scalar.activation(
+                    shifted[:],
+                    negated[:],
+                    mybir.ActivationFunctionType.Identity,
+                    bias=shift[:],
+                    scale=-1.0,
+                )
+            else:
+                nc.vector.tensor_scalar(
+                    shifted[:],
+                    negated[:],
+                    -1.0,
+                    shift[:],
+                    op0=mybir.AluOpType.mult,
+                    op1=mybir.AluOpType.add,
+                )
             nc.sync.dma_start(out[b * P : (b + 1) * P, :], shifted[:])

@@ -6,6 +6,7 @@ PIXELS = 512
 ANCHORS = 256
 BLOCKS = PIXELS // P
 INV_TEMPERATURE = 10.0
+DMA_ALIGN = 256
 
 FLOPS = 2 * P * PIXELS * ANCHORS
 
@@ -20,8 +21,8 @@ def tile_pixelcontrastloss_kernel(tc, table, w, offs, out):
         tc.psum_pool(name="psum", bufs=BLOCKS) as psum,
     ):
         offsets = held.tile([P, ANCHORS // 16], U16, name="offsets")
-        prototypes = held.tile([P, CLASSES], BF16, name="prototypes")
-        pixels = held.tile([P, PIXELS], BF16, name="pixels")
+        prototypes = held.tile([P, CLASSES], BF16, name="prototypes", align_bytes=DMA_ALIGN)
+        pixels = held.tile([P, PIXELS], BF16, name="pixels", align_bytes=DMA_ALIGN)
         nc.sync.dma_start(prototypes[:], table)
         nc.sync.dma_start(pixels[:, :P], w[:, :P])
         nc.sync.dma_start(offsets[:], offs)
@@ -48,7 +49,7 @@ def tile_pixelcontrastloss_kernel(tc, table, w, offs, out):
                 op1=mybir.AluOpType.min,
                 accum_out=shift[:],
             )
-            shifted = rows.tile([P, ANCHORS], F32, name="shifted")
+            shifted = rows.tile([P, ANCHORS], F32, name="shifted", align_bytes=DMA_ALIGN)
             if b < BLOCKS - 1:
                 nc.scalar.activation(
                     shifted[:],

@@ -6,7 +6,7 @@ PIXELS = 512
 ANCHORS = 256
 BLOCKS = PIXELS // P
 INV_TEMPERATURE = 10.0
-DMA_ALIGN = 256
+DMA_ALIGN = 1024
 
 FLOPS = 2 * P * PIXELS * ANCHORS
 
@@ -20,7 +20,7 @@ def tile_pixelcontrastloss_kernel(tc, table, w, offs, out):
         tc.tile_pool(name="rows", bufs=BLOCKS) as rows,
         tc.psum_pool(name="psum", bufs=BLOCKS) as psum,
     ):
-        offsets = held.tile([P, ANCHORS // 16], U16, name="offsets")
+        offsets = held.tile([P, ANCHORS // 16], U16, name="offsets", align_bytes=DMA_ALIGN)
         prototypes = held.tile([P, CLASSES], BF16, name="prototypes", align_bytes=DMA_ALIGN)
         pixels = held.tile([P, PIXELS], BF16, name="pixels", align_bytes=DMA_ALIGN)
         nc.sync.dma_start(prototypes[:], table)
@@ -38,8 +38,8 @@ def tile_pixelcontrastloss_kernel(tc, table, w, offs, out):
                 stop=True,
             )
 
-            negated = rows.tile([P, ANCHORS], F32, name="negated")
-            shift = rows.tile([P, 1], F32, name="shift")
+            negated = rows.tile([P, ANCHORS], F32, name="negated", align_bytes=DMA_ALIGN)
+            shift = rows.tile([P, 1], F32, name="shift", align_bytes=DMA_ALIGN)
             nc.vector.tensor_scalar(
                 negated[:],
                 product[:],

import concourse.mybir as mybir

P = 128
CLASSES = 512
PIXELS = 512
ANCHORS = 256
BLOCKS = PIXELS // P
INV_TEMPERATURE = 10.0
DMA_ALIGN = 1024

FLOPS = 2 * P * PIXELS * ANCHORS

BF16, F32, U16 = mybir.dt.bfloat16, mybir.dt.float32, mybir.dt.uint16


def tile_pixelcontrastloss_kernel(tc, table, w, offs, out):
    nc = tc.nc
    with (
        tc.tile_pool(name="held", bufs=1) as held,
        tc.tile_pool(name="rows", bufs=BLOCKS) as rows,
        tc.psum_pool(name="psum", bufs=BLOCKS) as psum,
    ):
        offsets = held.tile([P, ANCHORS // 16], U16, name="offsets", align_bytes=DMA_ALIGN)
        prototypes = held.tile([P, CLASSES], BF16, name="prototypes", align_bytes=DMA_ALIGN)
        pixels = held.tile([P, PIXELS], BF16, name="pixels", align_bytes=DMA_ALIGN)
        nc.sync.dma_start(prototypes[:], table)
        nc.sync.dma_start(pixels[:, :P], w[:, :P])
        nc.sync.dma_start(offsets[:], offs)
        nc.sync.dma_start(pixels[:, P:], w[:, P:])

        for b in range(BLOCKS):
            product = psum.tile([P, ANCHORS], F32, name="product")
            nc.tensor.matmul(
                product[:],
                pixels[:, b * P : (b + 1) * P],
                prototypes[:].indirect(offsets[:]),
                start=True,
                stop=True,
            )

            negated = rows.tile([P, ANCHORS], F32, name="negated", align_bytes=DMA_ALIGN)
            shift = rows.tile([P, 1], F32, name="shift", align_bytes=DMA_ALIGN)
            nc.vector.tensor_scalar(
                negated[:],
                product[:],
                -INV_TEMPERATURE,
                None,
                op0=mybir.AluOpType.mult,
                op1=mybir.AluOpType.min,
                accum_out=shift[:],
            )
            shifted = rows.tile([P, ANCHORS], F32, name="shifted", align_bytes=DMA_ALIGN)
            if b < BLOCKS - 1:
                nc.scalar.activation(
                    shifted[:],
                    negated[:],
                    mybir.ActivationFunctionType.Identity,
                    bias=shift[:],
                    scale=-1.0,
                )
            else:
                nc.vector.tensor_scalar(
                    shifted[:],
                    negated[:],
                    -1.0,
                    shift[:],
                    op0=mybir.AluOpType.mult,
                    op1=mybir.AluOpType.add,
                )
            nc.sync.dma_start(out[b * P : (b + 1) * P, :], shifted[:])
